import numpy as np
import ml_dtypes

BF16 = ml_dtypes.bfloat16


def bf(x):
    return np.asarray(x, np.float32).astype(BF16)


def f32(x):
    return np.asarray(x, np.float32)


def f64(x):
    return np.asarray(x).astype(np.float64)


def striped(idx):
    return np.tile(idx.reshape(-1, 16).T, (8, 1))


C, S, N, B, F, TMAX, RUN, HALF = 128, 256, 512, 128, 512, 128, 128, 64


def erf(a):
    c = np.clip(a, -6.0, 6.0)
    term = c.copy()
    total = c.copy()
    for n in range(1, 150):
        term = term * (2.0 * c * c) / (2.0 * n + 1.0)
        total = total + term
    return np.where(np.abs(a) > 6.0, np.sign(a), 2.0 / np.sqrt(np.pi) * np.exp(-c * c) * total)


def gelu_erf(v):
    return 0.5 * v * (1.0 + erf(v / np.sqrt(2.0)))


def time_features(t):
    freq = np.exp(np.arange(HALF, dtype=np.float32) * np.float32(-np.log(10000.0) / (HALF - 1)))
    ang = t.astype(np.float32)[None, :] * freq[:, None]
    return np.concatenate([np.sin(f64(ang)), np.cos(f64(ang))], 0)


def setup_inputs():
    t = np.random.permutation(TMAX)[:B]
    return {"tok": f32(np.random.standard_normal((C, S))), "lev": f32(0.5 * np.random.standard_normal((C, 1))), "tfeat": f32(time_features(t)), "w1": bf(np.random.standard_normal((C, F)) * np.sqrt(2.0 / C)), "b1": f32(0.1 * np.random.standard_normal((F, 1))), "w2": bf(np.random.standard_normal((F, C)) / np.sqrt(F)), "b2": f32(0.1 * np.random.standard_normal((C, 1))), "offs": striped(np.concatenate([np.random.permutation(S)[:RUN] for _ in range(N // RUN)]))}


def reference(tok, lev, tfeat, w1, b1, w2, b2, offs):
    idx = offs[:16].T.reshape(-1)
    hid = gelu_erf(f64(w1).T @ f64(tfeat) + f64(b1))
    cond = f64(w2).T @ hid + f64(b2) + f64(lev)
    return f64(tok)[:, idx] + np.tile(cond, (1, N // B))

@@ -1,0 +1,65 @@
+import concourse.mybir as mybir
+
+F32 = mybir.dt.float32
+BF16 = mybir.dt.bfloat16
+U16 = mybir.dt.uint16
+
+P = 128
+WORDS = 256
+N = 512
+SEQS = 128
+HIDDEN = 512
+BLOCKS = HIDDEN // P
+PIECES = N // SEQS
+
+FLOPS = 2 * P * HIDDEN * SEQS + 2 * HIDDEN * P * SEQS
+
+
+def tile_fractaldiffusionmodel_kernel(tc, tok, lev, tfeat, w1, b1, w2, b2, offs, out):
+    nc = tc.nc
+    add = mybir.AluOpType.add
+    gelu = mybir.ActivationFunctionType.Gelu
+
+    with (
+        tc.tile_pool(name="held", bufs=1) as held,
+        tc.psum_pool(name="psum", bufs=1) as psum,
+    ):
+        tfeat_f32 = held.tile([P, SEQS], F32, name="tfeat_f32")
+        nc.sync.dma_start(tfeat_f32[:], tfeat)
+        w1_sb = held.tile([P, HIDDEN], BF16, name="w1_sb")
+        nc.scalar.dma_start(w1_sb[:], w1)
+        b1_sb = held.tile([P, BLOCKS], F32, name="b1_sb")
+        w2_sb = held.tile([P, BLOCKS, P], BF16, name="w2_sb")
+        b2_sb = held.tile([P, 1], F32, name="b2_sb")
+        lev_sb = held.tile([P, 1], F32, name="lev_sb")
+        with nc.allow_non_contiguous_dma(reason="bias vectors, one element to a partition"):
+            nc.gpsimd.dma_start(b1_sb[:], b1.rearrange("(k p) o -> p (k o)", p=P))
+            nc.scalar.dma_start(w2_sb[:], w2.rearrange("(k p) c -> p k c", p=P))
+            nc.gpsimd.dma_start(b2_sb[:], b2)
+            nc.gpsimd.dma_start(lev_sb[:], lev)
+        offsets = held.tile([P, N // 16], U16, name="offsets")
+        nc.sync.dma_start(offsets[:], offs)
+        tok_sb = held.tile([P, WORDS], F32, name="tok_sb")
+        nc.sync.dma_start(tok_sb[:], tok)
+
+        tfeat_bf = held.tile([P, SEQS], BF16, name="tfeat_bf")
+        nc.vector.tensor_copy(tfeat_bf[:], tfeat_f32[:])
+
+        hid = held.tile([P, BLOCKS, SEQS], BF16, name="hid")
+        cond_ps = psum.tile([P, SEQS], F32, name="cond_ps")
+        for k in range(BLOCKS):
+            hid_ps = psum.tile([P, SEQS], F32, name=f"hid_ps{k}")
+            nc.tensor.matmul(hid_ps[:], w1_sb[:, k * P : (k + 1) * P], tfeat_bf[:], start=True, stop=True)
+            nc.scalar.activation(hid[:, k, :], hid_ps[:], gelu, bias=b1_sb[:, k : k + 1])
+        for k in range(BLOCKS):
+            nc.tensor.matmul(cond_ps[:], w2_sb[:, k, :], hid[:, k, :], start=(k == 0), stop=(k == BLOCKS - 1))
+
+        cond = held.tile([P, SEQS], F32, name="cond")
+        nc.vector.tensor_scalar(cond[:], cond_ps[:], b2_sb[:], lev_sb[:], add, add)
+
+        out_sb = held.tile([P, N], F32, name="out_sb")
+        for i in range(PIECES):
+            columns = slice(i * SEQS, (i + 1) * SEQS)
+            piece_offsets = offsets[:, i * (SEQS // 16) : (i + 1) * (SEQS // 16)]
+            nc.vector.tensor_tensor(out_sb[:, columns], tok_sb[:].indirect(piece_offsets), cond[:], add)
+            nc.sync.dma_start(out[:, columns], out_sb[:, columns])

@@ -24,6 +24,10 @@ def tile_fractaldiffusionmodel_kernel(tc, tok, lev, tfeat, w1, b1, w2, b2, offs,
         tc.tile_pool(name="held", bufs=1) as held,
         tc.psum_pool(name="psum", bufs=1) as psum,
     ):
+        warm = held.tile([P, 1], F32, name="warm")
+        nc.vector.memset(warm[:], 0.0)
+        nc.scalar.activation(warm[:], warm[:], gelu)
+
         tfeat_f32 = held.tile([P, SEQS], F32, name="tfeat_f32")
         nc.sync.dma_start(tfeat_f32[:], tfeat)
         w1_sb = held.tile([P, HIDDEN], BF16, name="w1_sb")

@@ -24,10 +24,6 @@ def tile_fractaldiffusionmodel_kernel(tc, tok, lev, tfeat, w1, b1, w2, b2, offs,
         tc.tile_pool(name="held", bufs=1) as held,
         tc.psum_pool(name="psum", bufs=1) as psum,
     ):
-        warm = held.tile([P, 1], F32, name="warm")
-        nc.vector.memset(warm[:], 0.0)
-        nc.scalar.activation(warm[:], warm[:], gelu)
-
         tfeat_f32 = held.tile([P, SEQS], F32, name="tfeat_f32")
         nc.sync.dma_start(tfeat_f32[:], tfeat)
         w1_sb = held.tile([P, HIDDEN], BF16, name="w1_sb")
@@ -37,14 +33,18 @@ def tile_fractaldiffusionmodel_kernel(tc, tok, lev, tfeat, w1, b1, w2, b2, offs,
         b2_sb = held.tile([P, 1], F32, name="b2_sb")
         lev_sb = held.tile([P, 1], F32, name="lev_sb")
         with nc.allow_non_contiguous_dma(reason="bias vectors, one element to a partition"):
-            nc.gpsimd.dma_start(b1_sb[:], b1.rearrange("(k p) o -> p (k o)", p=P))
+            nc.sync.dma_start(b1_sb[:], b1.rearrange("(k p) o -> p (k o)", p=P))
             nc.scalar.dma_start(w2_sb[:], w2.rearrange("(k p) c -> p k c", p=P))
-            nc.gpsimd.dma_start(b2_sb[:], b2)
-            nc.gpsimd.dma_start(lev_sb[:], lev)
+            nc.scalar.dma_start(b2_sb[:], b2)
+            nc.scalar.dma_start(lev_sb[:], lev)
         offsets = held.tile([P, N // 16], U16, name="offsets")
         nc.sync.dma_start(offsets[:], offs)
         tok_sb = held.tile([P, WORDS], F32, name="tok_sb")
         nc.sync.dma_start(tok_sb[:], tok)
+
+        warm = held.tile([P, 1], F32, name="warm")
+        nc.vector.memset(warm[:], 0.0)
+        nc.scalar.activation(warm[:], warm[:], gelu)
 
         tfeat_bf = held.tile([P, SEQS], BF16, name="tfeat_bf")
         nc.vector.tensor_copy(tfeat_bf[:], tfeat_f32[:])

@@ -28,19 +28,20 @@ def tile_fractaldiffusionmodel_kernel(tc, tok, lev, tfeat, w1, b1, w2, b2, offs,
         nc.sync.dma_start(tfeat_f32[:], tfeat)
         w1_sb = held.tile([P, HIDDEN], BF16, name="w1_sb")
         nc.scalar.dma_start(w1_sb[:], w1)
+        tok_sb = held.tile([P, WORDS], F32, name="tok_sb")
+        nc.scalar.dma_start(tok_sb[:], tok)
         b1_sb = held.tile([P, BLOCKS], F32, name="b1_sb")
         w2_sb = held.tile([P, BLOCKS, P], BF16, name="w2_sb")
+        with nc.allow_non_contiguous_dma(reason="hidden units in blocks of 128: short rows"):
+            nc.sync.dma_start(b1_sb[:], b1.rearrange("(k p) o -> p (k o)", p=P))
+            nc.sync.dma_start(w2_sb[:], w2.rearrange("(k p) c -> p k c", p=P))
+        offsets = held.tile([P, N // 16], U16, name="offsets")
+        nc.sync.dma_start(offsets[:], offs)
         b2_sb = held.tile([P, 1], F32, name="b2_sb")
         lev_sb = held.tile([P, 1], F32, name="lev_sb")
         with nc.allow_non_contiguous_dma(reason="bias vectors, one element to a partition"):
-            nc.sync.dma_start(b1_sb[:], b1.rearrange("(k p) o -> p (k o)", p=P))
-            nc.scalar.dma_start(w2_sb[:], w2.rearrange("(k p) c -> p k c", p=P))
-            nc.scalar.dma_start(b2_sb[:], b2)
-            nc.scalar.dma_start(lev_sb[:], lev)
-        offsets = held.tile([P, N // 16], U16, name="offsets")
-        nc.sync.dma_start(offsets[:], offs)
-        tok_sb = held.tile([P, WORDS], F32, name="tok_sb")
-        nc.sync.dma_start(tok_sb[:], tok)
+            nc.sync.dma_start(b2_sb[:], b2)
+            nc.sync.dma_start(lev_sb[:], lev)
 
         warm = held.tile([P, 1], F32, name="warm")
         nc.vector.memset(warm[:], 0.0)

@@ -28,20 +28,19 @@ def tile_fractaldiffusionmodel_kernel(tc, tok, lev, tfeat, w1, b1, w2, b2, offs,
         nc.sync.dma_start(tfeat_f32[:], tfeat)
         w1_sb = held.tile([P, HIDDEN], BF16, name="w1_sb")
         nc.scalar.dma_start(w1_sb[:], w1)
-        tok_sb = held.tile([P, WORDS], F32, name="tok_sb")
-        nc.scalar.dma_start(tok_sb[:], tok)
         b1_sb = held.tile([P, BLOCKS], F32, name="b1_sb")
         w2_sb = held.tile([P, BLOCKS, P], BF16, name="w2_sb")
-        with nc.allow_non_contiguous_dma(reason="hidden units in blocks of 128: short rows"):
-            nc.sync.dma_start(b1_sb[:], b1.rearrange("(k p) o -> p (k o)", p=P))
-            nc.sync.dma_start(w2_sb[:], w2.rearrange("(k p) c -> p k c", p=P))
-        offsets = held.tile([P, N // 16], U16, name="offsets")
-        nc.sync.dma_start(offsets[:], offs)
         b2_sb = held.tile([P, 1], F32, name="b2_sb")
         lev_sb = held.tile([P, 1], F32, name="lev_sb")
         with nc.allow_non_contiguous_dma(reason="bias vectors, one element to a partition"):
-            nc.sync.dma_start(b2_sb[:], b2)
-            nc.sync.dma_start(lev_sb[:], lev)
+            nc.sync.dma_start(b1_sb[:], b1.rearrange("(p k) o -> p (k o)", k=BLOCKS))
+            nc.scalar.dma_start(w2_sb[:], w2.rearrange("(p k) c -> p k c", k=BLOCKS))
+            nc.scalar.dma_start(b2_sb[:], b2)
+            nc.scalar.dma_start(lev_sb[:], lev)
+        offsets = held.tile([P, N // 16], U16, name="offsets")
+        nc.sync.dma_start(offsets[:], offs)
+        tok_sb = held.tile([P, WORDS], F32, name="tok_sb")
+        nc.sync.dma_start(tok_sb[:], tok)
 
         warm = held.tile([P, 1], F32, name="warm")
         nc.vector.memset(warm[:], 0.0)
@@ -51,10 +50,11 @@ def tile_fractaldiffusionmodel_kernel(tc, tok, lev, tfeat, w1, b1, w2, b2, offs,
         nc.vector.tensor_copy(tfeat_bf[:], tfeat_f32[:])
 
         hid = held.tile([P, BLOCKS, SEQS], BF16, name="hid")
+        w1_blocks = w1_sb[:].rearrange("d (p k) -> d k p", k=BLOCKS)
         cond_ps = psum.tile([P, SEQS], F32, name="cond_ps")
         for k in range(BLOCKS):
             hid_ps = psum.tile([P, SEQS], F32, name=f"hid_ps{k}")
-            nc.tensor.matmul(hid_ps[:], w1_sb[:, k * P : (k + 1) * P], tfeat_bf[:], start=True, stop=True)
+            nc.tensor.matmul(hid_ps[:], w1_blocks[:, k, :], tfeat_bf[:], start=True, stop=True)
             nc.scalar.activation(hid[:, k, :], hid_ps[:], gelu, bias=b1_sb[:, k : k + 1])
         for k in range(BLOCKS):
             nc.tensor.matmul(cond_ps[:], w2_sb[:, k, :], hid[:, k, :], start=(k == 0), stop=(k == BLOCKS - 1))

@@ -27,19 +27,19 @@ def tile_fractaldiffusionmodel_kernel(tc, tok, lev, tfeat, w1, b1, w2, b2, offs,
         tfeat_f32 = held.tile([P, SEQS], F32, name="tfeat_f32")
         nc.sync.dma_start(tfeat_f32[:], tfeat)
         w1_sb = held.tile([P, HIDDEN], BF16, name="w1_sb")
-        nc.scalar.dma_start(w1_sb[:], w1)
+        nc.sync.dma_start(w1_sb[:], w1)
         b1_sb = held.tile([P, BLOCKS], F32, name="b1_sb")
         w2_sb = held.tile([P, BLOCKS, P], BF16, name="w2_sb")
         b2_sb = held.tile([P, 1], F32, name="b2_sb")
         lev_sb = held.tile([P, 1], F32, name="lev_sb")
+        offsets = held.tile([P, N // 16], U16, name="offsets")
+        tok_sb = held.tile([P, WORDS], F32, name="tok_sb")
         with nc.allow_non_contiguous_dma(reason="bias vectors, one element to a partition"):
             nc.sync.dma_start(b1_sb[:], b1.rearrange("(p k) o -> p (k o)", k=BLOCKS))
-            nc.scalar.dma_start(w2_sb[:], w2.rearrange("(p k) c -> p k c", k=BLOCKS))
-            nc.scalar.dma_start(b2_sb[:], b2)
-            nc.scalar.dma_start(lev_sb[:], lev)
-        offsets = held.tile([P, N // 16], U16, name="offsets")
+            nc.sync.dma_start(w2_sb[:], w2.rearrange("(p k) c -> p k c", k=BLOCKS))
+            nc.sync.dma_start(b2_sb[:], b2)
+            nc.sync.dma_start(lev_sb[:], lev)
         nc.sync.dma_start(offsets[:], offs)
-        tok_sb = held.tile([P, WORDS], F32, name="tok_sb")
         nc.sync.dma_start(tok_sb[:], tok)
 
         warm = held.tile([P, 1], F32, name="warm")

@@ -46,6 +46,9 @@ def tile_fractaldiffusionmodel_kernel(tc, tok, lev, tfeat, w1, b1, w2, b2, offs,
         nc.vector.memset(warm[:], 0.0)
         nc.scalar.activation(warm[:], warm[:], gelu)
 
+        b2_lev = held.tile([P, 1], F32, name="b2_lev")
+        nc.vector.tensor_tensor(b2_lev[:], b2_sb[:], lev_sb[:], add)
+
         tfeat_bf = held.tile([P, SEQS], BF16, name="tfeat_bf")
         nc.vector.tensor_copy(tfeat_bf[:], tfeat_f32[:])
 
@@ -60,7 +63,7 @@ def tile_fractaldiffusionmodel_kernel(tc, tok, lev, tfeat, w1, b1, w2, b2, offs,
             nc.tensor.matmul(cond_ps[:], w2_sb[:, k, :], hid[:, k, :], start=(k == 0), stop=(k == BLOCKS - 1))
 
         cond = held.tile([P, SEQS], F32, name="cond")
-        nc.vector.tensor_scalar(cond[:], cond_ps[:], b2_sb[:], lev_sb[:], add, add)
+        nc.vector.tensor_scalar(cond[:], cond_ps[:], b2_lev[:], None, add)
 
         out_sb = held.tile([P, N], F32, name="out_sb")
         for i in range(PIECES):

@@ -11,6 +11,8 @@ SEQS = 128
 HIDDEN = 512
 BLOCKS = HIDDEN // P
 PIECES = N // SEQS
+HALF = SEQS // 2
+HALVES = (slice(0, HALF), slice(HALF, SEQS))
 
 FLOPS = 2 * P * HIDDEN * SEQS + 2 * HIDDEN * P * SEQS
 
@@ -54,19 +56,28 @@ def tile_fractaldiffusionmodel_kernel(tc, tok, lev, tfeat, w1, b1, w2, b2, offs,
 
         hid = held.tile([P, BLOCKS, SEQS], BF16, name="hid")
         w1_blocks = w1_sb[:].rearrange("d (p k) -> d k p", k=BLOCKS)
-        cond_ps = psum.tile([P, SEQS], F32, name="cond_ps")
+        cond_ps = [psum.tile([P, HALF], F32, name=f"cond_ps{h}") for h in range(2)]
         for k in range(BLOCKS):
             hid_ps = psum.tile([P, SEQS], F32, name=f"hid_ps{k}")
             nc.tensor.matmul(hid_ps[:], w1_blocks[:, k, :], tfeat_bf[:], start=True, stop=True)
-            nc.scalar.activation(hid[:, k, :], hid_ps[:], gelu, bias=b1_sb[:, k : k + 1])
+            for columns in HALVES if k == BLOCKS - 1 else (slice(0, SEQS),):
+                nc.scalar.activation(hid[:, k, columns], hid_ps[:, columns], gelu, bias=b1_sb[:, k : k + 1])
         for k in range(BLOCKS):
-            nc.tensor.matmul(cond_ps[:], w2_sb[:, k, :], hid[:, k, :], start=(k == 0), stop=(k == BLOCKS - 1))
+            for h in range(2):
+                nc.tensor.matmul(
+                    cond_ps[h][:], w2_sb[:, k, :], hid[:, k, HALVES[h]], start=(k == 0), stop=(k == BLOCKS - 1)
+                )
 
         cond = held.tile([P, SEQS], F32, name="cond")
-        nc.vector.tensor_scalar(cond[:], cond_ps[:], b2_lev[:], None, add)
+        for h in range(2):
+            nc.vector.tensor_scalar(cond[:, HALVES[h]], cond_ps[h][:], b2_lev[:], None, add)
 
         out_sb = held.tile([P, N], F32, name="out_sb")
-        for i in range(PIECES):
+        for h in range(2):
+            piece_offsets = offsets[:, h * (HALF // 16) : (h + 1) * (HALF // 16)]
+            nc.vector.tensor_tensor(out_sb[:, HALVES[h]], tok_sb[:].indirect(piece_offsets), cond[:, HALVES[h]], add)
+        nc.sync.dma_start(out[:, 0:SEQS], out_sb[:, 0:SEQS])
+        for i in range(1, PIECES):
             columns = slice(i * SEQS, (i + 1) * SEQS)
             piece_offsets = offsets[:, i * (SEQS // 16) : (i + 1) * (SEQS // 16)]
             nc.vector.tensor_tensor(out_sb[:, columns], tok_sb[:].indirect(piece_offsets), cond[:], add)

@@ -62,11 +62,18 @@ def tile_fractaldiffusionmodel_kernel(tc, tok, lev, tfeat, w1, b1, w2, b2, offs,
             nc.tensor.matmul(hid_ps[:], w1_blocks[:, k, :], tfeat_bf[:], start=True, stop=True)
             for columns in HALVES if k == BLOCKS - 1 else (slice(0, SEQS),):
                 nc.scalar.activation(hid[:, k, columns], hid_ps[:, columns], gelu, bias=b1_sb[:, k : k + 1])
-        for k in range(BLOCKS):
+
+        def add_block(k, h):
+            nc.tensor.matmul(
+                cond_ps[h][:], w2_sb[:, k, :], hid[:, k, HALVES[h]], start=(k == 0), stop=(k == BLOCKS - 1)
+            )
+
+        for k in range(BLOCKS - 2):
             for h in range(2):
-                nc.tensor.matmul(
-                    cond_ps[h][:], w2_sb[:, k, :], hid[:, k, HALVES[h]], start=(k == 0), stop=(k == BLOCKS - 1)
-                )
+                add_block(k, h)
+        for h in range(2):
+            for k in range(BLOCKS - 2, BLOCKS):
+                add_block(k, h)
 
         cond = held.tile([P, SEQS], F32, name="cond")
         for h in range(2):

@@ -13,6 +13,7 @@ BLOCKS = HIDDEN // P
 PIECES = N // SEQS
 HALF = SEQS // 2
 HALVES = (slice(0, HALF), slice(HALF, SEQS))
+WHOLE = (slice(0, SEQS),)
 
 FLOPS = 2 * P * HIDDEN * SEQS + 2 * HIDDEN * P * SEQS
 
@@ -52,15 +53,17 @@ def tile_fractaldiffusionmodel_kernel(tc, tok, lev, tfeat, w1, b1, w2, b2, offs,
         nc.vector.tensor_tensor(b2_lev[:], b2_sb[:], lev_sb[:], add)
 
         tfeat_bf = held.tile([P, SEQS], BF16, name="tfeat_bf")
-        nc.vector.tensor_copy(tfeat_bf[:], tfeat_f32[:])
+        for columns in HALVES:
+            nc.vector.tensor_copy(tfeat_bf[:, columns], tfeat_f32[:, columns])
 
         hid = held.tile([P, BLOCKS, SEQS], BF16, name="hid")
         w1_blocks = w1_sb[:].rearrange("d (p k) -> d k p", k=BLOCKS)
         cond_ps = [psum.tile([P, HALF], F32, name=f"cond_ps{h}") for h in range(2)]
         for k in range(BLOCKS):
             hid_ps = psum.tile([P, SEQS], F32, name=f"hid_ps{k}")
-            nc.tensor.matmul(hid_ps[:], w1_blocks[:, k, :], tfeat_bf[:], start=True, stop=True)
-            for columns in HALVES if k == BLOCKS - 1 else (slice(0, SEQS),):
+            for columns in HALVES if k == 0 else WHOLE:
+                nc.tensor.matmul(hid_ps[:, columns], w1_blocks[:, k, :], tfeat_bf[:, columns], start=True, stop=True)
+            for columns in HALVES if k == BLOCKS - 1 else WHOLE:
                 nc.scalar.activation(hid[:, k, columns], hid_ps[:, columns], gelu, bias=b1_sb[:, k : k + 1])
 
         def add_block(k, h):

import concourse.mybir as mybir

F32 = mybir.dt.float32
BF16 = mybir.dt.bfloat16
U16 = mybir.dt.uint16

P = 128
WORDS = 256
N = 512
SEQS = 128
HIDDEN = 512
BLOCKS = HIDDEN // P
PIECES = N // SEQS
HALF = SEQS // 2
HALVES = (slice(0, HALF), slice(HALF, SEQS))
WHOLE = (slice(0, SEQS),)

FLOPS = 2 * P * HIDDEN * SEQS + 2 * HIDDEN * P * SEQS


def tile_fractaldiffusionmodel_kernel(tc, tok, lev, tfeat, w1, b1, w2, b2, offs, out):
    nc = tc.nc
    add = mybir.AluOpType.add
    gelu = mybir.ActivationFunctionType.Gelu

    with (
        tc.tile_pool(name="held", bufs=1) as held,
        tc.psum_pool(name="psum", bufs=1) as psum,
    ):
        tfeat_f32 = held.tile([P, SEQS], F32, name="tfeat_f32")
        nc.sync.dma_start(tfeat_f32[:], tfeat)
        w1_sb = held.tile([P, HIDDEN], BF16, name="w1_sb")
        nc.sync.dma_start(w1_sb[:], w1)
        b1_sb = held.tile([P, BLOCKS], F32, name="b1_sb")
        w2_sb = held.tile([P, BLOCKS, P], BF16, name="w2_sb")
        b2_sb = held.tile([P, 1], F32, name="b2_sb")
        lev_sb = held.tile([P, 1], F32, name="lev_sb")
        offsets = held.tile([P, N // 16], U16, name="offsets")
        tok_sb = held.tile([P, WORDS], F32, name="tok_sb")
        with nc.allow_non_contiguous_dma(reason="bias vectors, one element to a partition"):
            nc.sync.dma_start(b1_sb[:], b1.rearrange("(p k) o -> p (k o)", k=BLOCKS))
            nc.sync.dma_start(w2_sb[:], w2.rearrange("(p k) c -> p k c", k=BLOCKS))
            nc.sync.dma_start(b2_sb[:], b2)
            nc.sync.dma_start(lev_sb[:], lev)
        nc.sync.dma_start(offsets[:], offs)
        nc.sync.dma_start(tok_sb[:], tok)

        warm = held.tile([P, 1], F32, name="warm")
        nc.vector.memset(warm[:], 0.0)
        nc.scalar.activation(warm[:], warm[:], gelu)

        b2_lev = held.tile([P, 1], F32, name="b2_lev")
        nc.vector.tensor_tensor(b2_lev[:], b2_sb[:], lev_sb[:], add)

        tfeat_bf = held.tile([P, SEQS], BF16, name="tfeat_bf")
        for columns in HALVES:
            nc.vector.tensor_copy(tfeat_bf[:, columns], tfeat_f32[:, columns])

        hid = held.tile([P, BLOCKS, SEQS], BF16, name="hid")
        w1_blocks = w1_sb[:].rearrange("d (p k) -> d k p", k=BLOCKS)
        cond_ps = [psum.tile([P, HALF], F32, name=f"cond_ps{h}") for h in range(2)]
        for k in range(BLOCKS):
            hid_ps = psum.tile([P, SEQS], F32, name=f"hid_ps{k}")
            for columns in HALVES if k == 0 else WHOLE:
                nc.tensor.matmul(hid_ps[:, columns], w1_blocks[:, k, :], tfeat_bf[:, columns], start=True, stop=True)
            for columns in HALVES if k == BLOCKS - 1 else WHOLE:
                nc.scalar.activation(hid[:, k, columns], hid_ps[:, columns], gelu, bias=b1_sb[:, k : k + 1])

        def add_block(k, h):
            nc.tensor.matmul(
                cond_ps[h][:], w2_sb[:, k, :], hid[:, k, HALVES[h]], start=(k == 0), stop=(k == BLOCKS - 1)
            )

        for k in range(BLOCKS - 2):
            for h in range(2):
                add_block(k, h)
        for h in range(2):
            for k in range(BLOCKS - 2, BLOCKS):
                add_block(k, h)

        cond = held.tile([P, SEQS], F32, name="cond")
        for h in range(2):
            nc.vector.tensor_scalar(cond[:, HALVES[h]], cond_ps[h][:], b2_lev[:], None, add)

        out_sb = held.tile([P, N], F32, name="out_sb")
        for h in range(2):
            piece_offsets = offsets[:, h * (HALF // 16) : (h + 1) * (HALF // 16)]
            nc.vector.tensor_tensor(out_sb[:, HALVES[h]], tok_sb[:].indirect(piece_offsets), cond[:, HALVES[h]], add)
        nc.sync.dma_start(out[:, 0:SEQS], out_sb[:, 0:SEQS])
        for i in range(1, PIECES):
            columns = slice(i * SEQS, (i + 1) * SEQS)
            piece_offsets = offsets[:, i * (SEQS // 16) : (i + 1) * (SEQS // 16)]
            nc.vector.tensor_tensor(out_sb[:, columns], tok_sb[:].indirect(piece_offsets), cond[:], add)
            nc.sync.dma_start(out[:, columns], out_sb[:, columns])
